import numpy as np
import ml_dtypes


def mxq(x, axis, fmt="e4m3"):
    dtype, down = {"e4m3": (ml_dtypes.float8_e4m3fn, 7), "e5m2": (ml_dtypes.float8_e5m2, 14)}[fmt]
    v = np.moveaxis(np.asarray(x, np.float32).astype(ml_dtypes.bfloat16).astype(np.float64), axis, -1)
    blocks = v.reshape(v.shape[:-1] + (-1, 32))
    amax = np.abs(blocks).max(-1, keepdims=True)
    byte = np.maximum(np.where(amax > 0, np.frexp(amax)[1] - 1 + 127, 0) - down, 1)
    scale = np.exp2(byte - 127.0)
    codes = (blocks / scale).astype(np.float32).astype(dtype).astype(np.float64)
    return np.moveaxis((codes * scale).reshape(v.shape), -1, axis)


WIDE = False


def mx_kscale(k):
    if not WIDE:
        return np.ones(k)
    levels = np.array([10, -10, 5, -5, 0])
    a = np.random.permutation(np.resize(levels, k // 512 * 4)).reshape(k // 512, 4)
    idx = np.arange(k)
    return np.exp2(a[idx // 512, idx % 128 // 32])


BF16 = ml_dtypes.bfloat16


def bf(x):
    return np.asarray(x, np.float32).astype(BF16)


def f64(x):
    return np.asarray(x).astype(np.float64)


B, T, D, E, F, H = 2, 128, 1024, 8, 512, 256
N = B * T
EF = E * F


def silu(v):
    return v / (1.0 + np.exp(-v))


def setup_inputs():
    s = mx_kscale(D)
    t = mx_kscale(EF).reshape(E, F)
    er = np.exp(np.random.standard_normal((N, E)))
    return {"x": bf(np.random.standard_normal((B, T, D)) * s),
            "r": bf(er / er.sum(-1, keepdims=True)),
            "Wg": bf(np.random.standard_normal((E, D, F)) / np.sqrt(D) / s[None, :, None]),
            "Wu": bf(np.random.standard_normal((E, D, F)) / np.sqrt(D) / s[None, :, None] * t[:, None, :]),
            "Wd": bf(np.random.standard_normal((E, F, D)) * 1.5 / np.sqrt(F) / t[:, :, None])}


def reference(x, r, Wg, Wu, Wd):
    xq = mxq(f64(x).reshape(N, D), 1, "e4m3")
    g = silu(xq @ mxq(f64(Wg), 1, "e4m3"))
    u = xq @ mxq(f64(Wu), 1, "e4m3")
    w = f64(r).T[:, :, None] * (g * u)
    w = np.swapaxes(w, 0, 1).reshape(N, EF)
    y = mxq(w, 1, "e4m3") @ mxq(f64(Wd).reshape(EF, D), 0, "e4m3")
    return y.reshape(B, T, D)

@@ -1,0 +1,265 @@
+from contextlib import ExitStack
+
+import concourse.mybir as mybir
+from concourse.masks import make_identity
+
+F32 = mybir.dt.float32
+BF16 = mybir.dt.bfloat16
+U32 = mybir.dt.uint32
+U8 = mybir.dt.uint8
+FP8X4 = mybir.dt.float8_e4m3fn_x4
+SILU = mybir.ActivationFunctionType.Silu
+MULT = mybir.AluOpType.mult
+
+P = 128
+E = 8
+D = 1024
+F = 512
+NTOK = 256
+FLOPS = 2 * NTOK * D * F * E * 2 + 2 * NTOK * E * F * D
+
+N1 = 32
+N2 = 16
+NU = N1 + N2
+RAW_BUFS = 16
+CV1 = 280
+CV2 = 248
+MANUAL = True
+
+
+def tile_moelayer_pa_kernel(tc, x, r, Wg, Wu, Wd, out):
+    nc = tc.nc
+    with ExitStack() as ctx:
+        const = ctx.enter_context(tc.tile_pool(name="const", bufs=1))
+        rawa = ctx.enter_context(tc.tile_pool(name="rawa", bufs=RAW_BUFS))
+        rawd = ctx.enter_context(tc.tile_pool(name="rawd", bufs=E))
+        grp = ctx.enter_context(tc.tile_pool(name="grp", bufs=5))
+        cod = ctx.enter_context(tc.tile_pool(name="cod", bufs=6))
+        act = ctx.enter_context(tc.tile_pool(name="act", bufs=3))
+        yst = ctx.enter_context(tc.tile_pool(name="yst", bufs=4))
+        psg = ctx.enter_context(tc.psum_pool(name="psg", bufs=3))
+        psu = ctx.enter_context(tc.psum_pool(name="psu", bufs=3))
+        pst = ctx.enter_context(tc.psum_pool(name="pst", bufs=2))
+        if MANUAL:
+            ctx.enter_context(tc.manual_schedule())
+
+        raw_tiles = {}
+        grp_tiles = {}
+        code_tiles = {}
+        acc = {}
+        sg_tiles = {}
+        w_tiles = {}
+        wt_tiles = {}
+        wg_tiles = {}
+
+        def load(n):
+            if n < N1:
+                e, i = divmod(n, 4)
+                src = (Wg if i < 2 else Wu)[e]
+                c = i % 2
+                t = rawa.tile([P, 4, F], BF16, name="rawa", tag="rawa")
+                nc.sync.dma_start(
+                    out=t[:], in_=src[512 * c : 512 * c + 512, :].rearrange("(p j) f -> p j f", j=4)
+                )
+                raw_tiles[n] = t
+            else:
+                e = n - N1
+                t = rawd.tile([P, 4, D], BF16, name="rawd", tag="rawd")
+                nc.sync.dma_start(out=t[:], in_=Wd[e].rearrange("(t p) d -> p t d", t=4))
+                raw_tiles[n] = t
+
+        def source(n):
+            if n < N1:
+                return raw_tiles[n][:]
+            h, e = divmod(n - N1, E)
+            return raw_tiles[N1 + e][:, :, 512 * h : 512 * h + 512]
+
+        def regroup(n):
+            g = grp.tile([P, F, 4], BF16, name="grp", tag="grp", align_bytes=64)
+            grp_tiles[n] = g
+            src = source(n)
+            cv = CV1 if n < N1 else CV2
+            nc.scalar.copy(
+                out=g[:, cv:F, :].rearrange("p (c i) t -> p c t i", i=4),
+                in_=src[:, :, cv:F].rearrange("p t (c i) -> p c t i", i=4),
+            )
+            nc.vector.tensor_copy(
+                out=g[:, 0:cv, :].rearrange("p (c i) t -> p c t i", i=4),
+                in_=src[:, :, 0:cv].rearrange("p t (c i) -> p c t i", i=4),
+            )
+
+        def quantise(n):
+            codes = cod.tile([P, F], U32, name="codes", tag="codes", align_bytes=64)
+            plane = cod.tile([P, F], U8, name="plane", tag="plane", align_bytes=64)
+            nc.vector.quantize_mx(
+                out=codes[:].bitcast(FP8X4),
+                scales=plane[:],
+                in_=grp_tiles[n][:].rearrange("p w t -> p (w t)"),
+            )
+            code_tiles[n] = (codes, plane)
+
+        ident_f = const.tile([P, P], F32, name="ident_f")
+        make_identity(nc, ident_f[:])
+        ident_b = const.tile([P, P], BF16, name="ident_b")
+        make_identity(nc, ident_b[:])
+        r_sb = const.tile([P, 2, E], BF16, name="r_sb")
+        nc.scalar.dma_start(out=r_sb[:], in_=r.rearrange("(a p) e -> p a e", a=2))
+        warm = const.tile([P, 1], F32, name="warm")
+        nc.vector.memset(warm[:], 0.0)
+        nc.scalar.activation(out=warm[:], in_=warm[:], func=SILU)
+        x_sb = const.tile([P, 2, D], BF16, name="x_sb")
+        load(0)
+        nc.sync.dma_start(out=x_sb[:], in_=x.rearrange("b t d -> t b d"))
+        for n in range(1, RAW_BUFS):
+            load(n)
+
+        r32 = const.tile([P, 2, E], F32, name="r32")
+        nc.vector.tensor_copy(out=r32[:], in_=r_sb[:])
+
+        xg = const.tile([P, 2, NTOK, 4], BF16, name="xg", align_bytes=64)
+        xc = const.tile([P, 2 * NTOK], U32, name="xc", align_bytes=64)
+        xs = const.tile([P, 2 * NTOK], U8, name="xs", align_bytes=64)
+        wc = const.tile([P, E, NTOK], U32, name="wc", align_bytes=64)
+        ws = const.tile([P, E, NTOK], U8, name="ws", align_bytes=64)
+
+        def x_transposes():
+            xw = x_sb[:].bitcast(F32).rearrange("p a (c q u) -> p a c u q", c=2, u=2)
+            xg32 = xg[:].bitcast(F32)
+            for c in range(2):
+                xt = pst.tile([P, 2, 2, P], F32, name="xt", tag="tp")
+                for a in range(2):
+                    for u in range(2):
+                        nc.tensor.transpose(out=xt[:, a, u, :], in_=xw[:, a, c, u, :], identity=ident_f[:])
+                nc.scalar.copy(
+                    out=xg32[:, c].rearrange("p (a q) u -> p a q u", a=2),
+                    in_=xt[:].rearrange("p a u q -> p a q u"),
+                )
+
+        def x_quantise():
+            nc.vector.quantize_mx(
+                out=xc[:].bitcast(FP8X4),
+                scales=xs[:],
+                in_=xg[:].rearrange("p c n t -> p (c n t)"),
+            )
+
+        def matmuls(n):
+            codes, plane = code_tiles[n]
+            if n < N1:
+                e, i = divmod(n, 4)
+                c = i % 2
+                for a in range(2):
+                    if c == 0:
+                        pool = psg if i < 2 else psu
+                        acc[(i // 2, e, a)] = pool.tile([P, F], F32, name="acc", tag="acc")
+                    cols = slice(NTOK * c + P * a, NTOK * c + P * a + P)
+                    nc.tensor.matmul_mx(
+                        out=acc[(i // 2, e, a)][:],
+                        lhsT=xc[:, cols].bitcast(FP8X4),
+                        lhsT_scale=xs[:, cols],
+                        rhs=codes[:].bitcast(FP8X4),
+                        rhs_scale=plane[:],
+                        start=(c == 0),
+                        stop=(c == 1),
+                    )
+            else:
+                h, e = divmod(n - N1, E)
+                for a in range(2):
+                    if e == 0:
+                        pool = psg if h == 0 else psu
+                        acc[(2 + h, 0, a)] = pool.tile([P, F], F32, name="acc", tag="acc")
+                    cols = slice(P * a, P * a + P)
+                    nc.tensor.matmul_mx(
+                        out=acc[(2 + h, 0, a)][:],
+                        lhsT=wc[:, e, cols].bitcast(FP8X4),
+                        lhsT_scale=ws[:, e, cols],
+                        rhs=codes[:].bitcast(FP8X4),
+                        rhs_scale=plane[:],
+                        start=(e == 0),
+                        stop=(e == E - 1),
+                    )
+
+        def silu(e, a):
+            sg = act.tile([P, F], F32, name="sg", tag="sg")
+            nc.scalar.activation(out=sg[:], in_=acc[(0, e, a)][:], func=SILU)
+            sg_tiles[(e, a)] = sg
+
+        def combine(e, a):
+            w = act.tile([P, F], BF16, name="w", tag="w")
+            nc.vector.scalar_tensor_tensor(
+                out=w[:],
+                in0=sg_tiles[(e, a)][:],
+                scalar=r32[:, a, e : e + 1],
+                in1=acc[(1, e, a)][:],
+                op0=MULT,
+                op1=MULT,
+            )
+            w_tiles[(e, a)] = w
+
+        def w_transposes(e):
+            wt = pst.tile([P, 2, 4, P], BF16, name="wt", tag="tp")
+            for a in range(2):
+                for t in range(4):
+                    nc.tensor.transpose(
+                        out=wt[:, a, t, :], in_=w_tiles[(e, a)][:, P * t : P * t + P], identity=ident_b[:]
+                    )
+            wt_tiles[e] = wt
+
+        def w_copy(e, a):
+            if a == 0:
+                wg_tiles[e] = act.tile([P, NTOK, 4], BF16, name="wg", tag="wg", align_bytes=64)
+            nc.scalar.copy(
+                out=wg_tiles[e][:, P * a : P * a + P, :],
+                in_=wt_tiles[e][:, a].rearrange("p t q -> p q t"),
+            )
+
+        def w_quantise(e):
+            nc.vector.quantize_mx(
+                out=wc[:, e, :].bitcast(FP8X4),
+                scales=ws[:, e, :],
+                in_=wg_tiles[e][:].rearrange("p n t -> p (n t)"),
+            )
+
+        def y_out(h, a, copy, queue):
+            y = yst.tile([P, F], F32, name="y", tag="y")
+            copy(out=y[:], in_=acc[(2 + h, 0, a)][:])
+            queue.dma_start(out=out[a][:, 512 * h : 512 * h + 512], in_=y[:])
+
+        for n in range(-2, NU):
+            m = n + 2
+            if m < NU:
+                regroup(m)
+                nxt = m + RAW_BUFS
+                if nxt < N1:
+                    load(nxt)
+                elif nxt == N1:
+                    for e in range(E):
+                        load(N1 + e)
+            if n == -2:
+                x_transposes()
+            if n == -1:
+                x_quantise()
+            if n < 0:
+                continue
+            quantise(n)
+            if n % 4 == 3 and 11 <= n <= 39:
+                w_quantise((n - 11) // 4)
+            matmuls(n)
+            if n < N1 and n % 4 == 2:
+                silu(n // 4, 0)
+            if n < N1 and n % 4 == 3:
+                silu(n // 4, 1)
+            if n % 4 == 0 and 8 <= n <= 36:
+                w_copy((n - 8) // 4, 0)
+            if n % 4 == 1 and 9 <= n <= 37:
+                w_copy((n - 9) // 4, 1)
+            if n == 40:
+                y_out(0, 0, nc.scalar.copy, nc.sync)
+            if n == 41:
+                y_out(0, 1, nc.scalar.copy, nc.sync)
+            if n % 4 == 1 and 5 <= n <= 33:
+                combine((n - 5) // 4, 0)
+            if n % 4 == 2 and 6 <= n <= 34:
+                combine((n - 6) // 4, 1)
+                w_transposes((n - 6) // 4)
+        y_out(1, 0, nc.vector.tensor_copy, nc.sync)
+        y_out(1, 1, nc.scalar.copy, nc.scalar)

@@ -19,11 +19,11 @@ NTOK = 256
 FLOPS = 2 * NTOK * D * F * E * 2 + 2 * NTOK * E * F * D
 
 N1 = 32
-N2 = 16
-NU = N1 + N2
+BLOCKS = ((0, 512), (512, 256), (768, 256))
+NU = N1 + E * len(BLOCKS)
 RAW_BUFS = 16
 CV1 = 280
-CV2 = 248
+CV2 = {512: 256, 256: 128}
 MANUAL = True
 
 
@@ -33,10 +33,10 @@ def tile_moelayer_pa_kernel(tc, x, r, Wg, Wu, Wd, out):
         const = ctx.enter_context(tc.tile_pool(name="const", bufs=1))
         rawa = ctx.enter_context(tc.tile_pool(name="rawa", bufs=RAW_BUFS))
         rawd = ctx.enter_context(tc.tile_pool(name="rawd", bufs=E))
-        grp = ctx.enter_context(tc.tile_pool(name="grp", bufs=5))
-        cod = ctx.enter_context(tc.tile_pool(name="cod", bufs=6))
+        grp = ctx.enter_context(tc.tile_pool(name="grp", bufs=6))
+        cod = ctx.enter_context(tc.tile_pool(name="cod", bufs=8))
         act = ctx.enter_context(tc.tile_pool(name="act", bufs=3))
-        yst = ctx.enter_context(tc.tile_pool(name="yst", bufs=4))
+        yst = ctx.enter_context(tc.tile_pool(name="yst", bufs=6))
         psg = ctx.enter_context(tc.psum_pool(name="psg", bufs=3))
         psu = ctx.enter_context(tc.psum_pool(name="psu", bufs=3))
         pst = ctx.enter_context(tc.psum_pool(name="pst", bufs=2))
@@ -68,29 +68,39 @@ def tile_moelayer_pa_kernel(tc, x, r, Wg, Wu, Wd, out):
                 nc.sync.dma_start(out=t[:], in_=Wd[e].rearrange("(t p) d -> p t d", t=4))
                 raw_tiles[n] = t
 
+        def width(n):
+            return F if n < N1 else BLOCKS[(n - N1) // E][1]
+
         def source(n):
             if n < N1:
                 return raw_tiles[n][:]
-            h, e = divmod(n - N1, E)
-            return raw_tiles[N1 + e][:, :, 512 * h : 512 * h + 512]
+            b, e = divmod(n - N1, E)
+            return raw_tiles[N1 + e][:, :, BLOCKS[b][0] : BLOCKS[b][0] + BLOCKS[b][1]]
 
         def regroup(n):
-            g = grp.tile([P, F, 4], BF16, name="grp", tag="grp", align_bytes=64)
+            w = width(n)
+            g = grp.tile([P, w, 4], BF16, name="grp", tag="grp", align_bytes=64)
             grp_tiles[n] = g
             src = source(n)
-            cv = CV1 if n < N1 else CV2
+            cv = CV1 if n < N1 else CV2[w]
             nc.scalar.copy(
-                out=g[:, cv:F, :].rearrange("p (c i) t -> p c t i", i=4),
-                in_=src[:, :, cv:F].rearrange("p t (c i) -> p c t i", i=4),
+                out=g[:, cv:w, :].rearrange("p (c i) t -> p c t i", i=4),
+                in_=src[:, :, cv:w].rearrange("p t (c i) -> p c t i", i=4),
             )
             nc.vector.tensor_copy(
                 out=g[:, 0:cv, :].rearrange("p (c i) t -> p c t i", i=4),
                 in_=src[:, :, 0:cv].rearrange("p t (c i) -> p c t i", i=4),
             )
+            nxt = n + RAW_BUFS
+            if nxt < N1:
+                load(nxt)
+            elif nxt == N1:
+                for e in range(E):
+                    load(N1 + e)
 
         def quantise(n):
-            codes = cod.tile([P, F], U32, name="codes", tag="codes", align_bytes=64)
-            plane = cod.tile([P, F], U8, name="plane", tag="plane", align_bytes=64)
+            codes = cod.tile([P, width(n)], U32, name="codes", tag="codes", align_bytes=64)
+            plane = cod.tile([P, width(n)], U8, name="plane", tag="plane", align_bytes=64)
             nc.vector.quantize_mx(
                 out=codes[:].bitcast(FP8X4),
                 scales=plane[:],
@@ -122,18 +132,17 @@ def tile_moelayer_pa_kernel(tc, x, r, Wg, Wu, Wd, out):
         wc = const.tile([P, E, NTOK], U32, name="wc", align_bytes=64)
         ws = const.tile([P, E, NTOK], U8, name="ws", align_bytes=64)
 
-        def x_transposes():
+        def x_transposes(c):
             xw = x_sb[:].bitcast(F32).rearrange("p a (c q u) -> p a c u q", c=2, u=2)
             xg32 = xg[:].bitcast(F32)
-            for c in range(2):
-                xt = pst.tile([P, 2, 2, P], F32, name="xt", tag="tp")
-                for a in range(2):
-                    for u in range(2):
-                        nc.tensor.transpose(out=xt[:, a, u, :], in_=xw[:, a, c, u, :], identity=ident_f[:])
-                nc.scalar.copy(
-                    out=xg32[:, c].rearrange("p (a q) u -> p a q u", a=2),
-                    in_=xt[:].rearrange("p a u q -> p a q u"),
-                )
+            xt = pst.tile([P, 2, 2, P], F32, name="xt", tag="tp")
+            for a in range(2):
+                for u in range(2):
+                    nc.tensor.transpose(out=xt[:, a, u, :], in_=xw[:, a, c, u, :], identity=ident_f[:])
+            nc.scalar.copy(
+                out=xg32[:, c].rearrange("p (a q) u -> p a q u", a=2),
+                in_=xt[:].rearrange("p a u q -> p a q u"),
+            )
 
         def x_quantise():
             nc.vector.quantize_mx(
@@ -162,14 +171,14 @@ def tile_moelayer_pa_kernel(tc, x, r, Wg, Wu, Wd, out):
                         stop=(c == 1),
                     )
             else:
-                h, e = divmod(n - N1, E)
+                b, e = divmod(n - N1, E)
                 for a in range(2):
                     if e == 0:
-                        pool = psg if h == 0 else psu
-                        acc[(2 + h, 0, a)] = pool.tile([P, F], F32, name="acc", tag="acc")
+                        pool = (psg, psu, (psg, psu)[a])[b]
+                        acc[(2 + b, 0, a)] = pool.tile([P, BLOCKS[b][1]], F32, name="acc", tag="acc")
                     cols = slice(P * a, P * a + P)
                     nc.tensor.matmul_mx(
-                        out=acc[(2 + h, 0, a)][:],
+                        out=acc[(2 + b, 0, a)][:],
                         lhsT=wc[:, e, cols].bitcast(FP8X4),
                         lhsT_scale=ws[:, e, cols],
                         rhs=codes[:].bitcast(FP8X4),
@@ -219,31 +228,29 @@ def tile_moelayer_pa_kernel(tc, x, r, Wg, Wu, Wd, out):
                 in_=wg_tiles[e][:].rearrange("p n t -> p (n t)"),
             )
 
-        def y_out(h, a, copy, queue):
-            y = yst.tile([P, F], F32, name="y", tag="y")
-            copy(out=y[:], in_=acc[(2 + h, 0, a)][:])
-            queue.dma_start(out=out[a][:, 512 * h : 512 * h + 512], in_=y[:])
+        def y_out(b, a, copy, queue):
+            y = yst.tile([P, BLOCKS[b][1]], F32, name="y", tag="y")
+            copy(out=y[:], in_=acc[(2 + b, 0, a)][:])
+            queue.dma_start(out=out[a][:, BLOCKS[b][0] : BLOCKS[b][0] + BLOCKS[b][1]], in_=y[:])
 
-        for n in range(-2, NU):
-            m = n + 2
-            if m < NU:
-                regroup(m)
-                nxt = m + RAW_BUFS
-                if nxt < N1:
-                    load(nxt)
-                elif nxt == N1:
-                    for e in range(E):
-                        load(N1 + e)
-            if n == -2:
-                x_transposes()
-            if n == -1:
-                x_quantise()
+        regrouped = 0
+        for n in range(-1, NU):
+            ahead = 1 if n < 0 else min(n, 2)
+            while regrouped <= min(n + ahead, NU - 1):
+                regroup(regrouped)
+                if regrouped < 2:
+                    x_transposes(regrouped)
+                regrouped += 1
             if n < 0:
                 continue
             quantise(n)
+            if n == 1:
+                x_quantise()
+                matmuls(0)
             if n % 4 == 3 and 11 <= n <= 39:
                 w_quantise((n - 11) // 4)
-            matmuls(n)
+            if n >= 1:
+                matmuls(n)
             if n < N1 and n % 4 == 2:
                 silu(n // 4, 0)
             if n < N1 and n % 4 == 3:
@@ -252,14 +259,15 @@ def tile_moelayer_pa_kernel(tc, x, r, Wg, Wu, Wd, out):
                 w_copy((n - 8) // 4, 0)
             if n % 4 == 1 and 9 <= n <= 37:
                 w_copy((n - 9) // 4, 1)
-            if n == 40:
-                y_out(0, 0, nc.scalar.copy, nc.sync)
-            if n == 41:
-                y_out(0, 1, nc.scalar.copy, nc.sync)
+            for b in range(len(BLOCKS) - 1):
+                if n == N1 + E * b + E:
+                    y_out(b, 0, nc.scalar.copy, nc.sync)
+                if n == N1 + E * b + E + 1:
+                    y_out(b, 1, nc.scalar.copy, nc.sync)
             if n % 4 == 1 and 5 <= n <= 33:
                 combine((n - 5) // 4, 0)
             if n % 4 == 2 and 6 <= n <= 34:
                 combine((n - 6) // 4, 1)
                 w_transposes((n - 6) // 4)
-        y_out(1, 0, nc.vector.tensor_copy, nc.sync)
-        y_out(1, 1, nc.scalar.copy, nc.scalar)
+        y_out(len(BLOCKS) - 1, 0, nc.vector.tensor_copy, nc.sync)
+        y_out(len(BLOCKS) - 1, 1, nc.scalar.copy, nc.scalar)

@@ -22,8 +22,11 @@ N1 = 32
 BLOCKS = ((0, 512), (512, 256), (768, 256))
 NU = N1 + E * len(BLOCKS)
 RAW_BUFS = 16
-CV1 = 280
+CV1 = 240
 CV2 = {512: 256, 256: 128}
+CV2_PE = 208
+N_PE = 38
+PE_COLS = 128
 MANUAL = True
 
 
@@ -37,9 +40,10 @@ def tile_moelayer_pa_kernel(tc, x, r, Wg, Wu, Wd, out):
         cod = ctx.enter_context(tc.tile_pool(name="cod", bufs=8))
         act = ctx.enter_context(tc.tile_pool(name="act", bufs=3))
         yst = ctx.enter_context(tc.tile_pool(name="yst", bufs=6))
-        psg = ctx.enter_context(tc.psum_pool(name="psg", bufs=3))
-        psu = ctx.enter_context(tc.psum_pool(name="psu", bufs=3))
-        pst = ctx.enter_context(tc.psum_pool(name="pst", bufs=2))
+        psg = ctx.enter_context(tc.psum_pool(name="psg", bufs=2))
+        psu = ctx.enter_context(tc.psum_pool(name="psu", bufs=2))
+        pst = ctx.enter_context(tc.psum_pool(name="pst", bufs=1))
+        psc = ctx.enter_context(tc.psum_pool(name="psc", bufs=3))
         if MANUAL:
             ctx.enter_context(tc.manual_schedule())
 
@@ -51,6 +55,7 @@ def tile_moelayer_pa_kernel(tc, x, r, Wg, Wu, Wd, out):
         w_tiles = {}
         wt_tiles = {}
         wg_tiles = {}
+        ck_tiles = {}
 
         def load(n):
             if n < N1:
@@ -77,16 +82,34 @@ def tile_moelayer_pa_kernel(tc, x, r, Wg, Wu, Wd, out):
             b, e = divmod(n - N1, E)
             return raw_tiles[N1 + e][:, :, BLOCKS[b][0] : BLOCKS[b][0] + BLOCKS[b][1]]
 
+        def split(n):
+            return CV1 if n < N1 else (CV2_PE if n < N_PE else CV2[width(n)])
+
+        def pe_regroup(n):
+            cv = split(n)
+            ck = psc.tile([P, PE_COLS, 4], BF16, name="ck", tag="ck")
+            nc.tensor.matmul(
+                out=ck[:].rearrange("p w t -> p t w"),
+                lhsT=ident_b[:],
+                rhs=source(n)[:, :, cv : cv + PE_COLS],
+                start=True,
+                stop=True,
+            )
+            ck_tiles[n] = ck
+
         def regroup(n):
             w = width(n)
             g = grp.tile([P, w, 4], BF16, name="grp", tag="grp", align_bytes=64)
             grp_tiles[n] = g
             src = source(n)
-            cv = CV1 if n < N1 else CV2[w]
+            cv = split(n)
+            cs = cv + PE_COLS if n < N_PE else cv
             nc.scalar.copy(
-                out=g[:, cv:w, :].rearrange("p (c i) t -> p c t i", i=4),
-                in_=src[:, :, cv:w].rearrange("p t (c i) -> p c t i", i=4),
+                out=g[:, cs:w, :].rearrange("p (c i) t -> p c t i", i=4),
+                in_=src[:, :, cs:w].rearrange("p t (c i) -> p c t i", i=4),
             )
+            if n < N_PE:
+                nc.scalar.copy(out=g[:, cv:cs, :], in_=ck_tiles[n][:])
             nc.vector.tensor_copy(
                 out=g[:, 0:cv, :].rearrange("p (c i) t -> p c t i", i=4),
                 in_=src[:, :, 0:cv].rearrange("p t (c i) -> p c t i", i=4),
@@ -174,7 +197,7 @@ def tile_moelayer_pa_kernel(tc, x, r, Wg, Wu, Wd, out):
                 b, e = divmod(n - N1, E)
                 for a in range(2):
                     if e == 0:
-                        pool = (psg, psu, (psg, psu)[a])[b]
+                        pool = (psg, psu, psg)[b]
                         acc[(2 + b, 0, a)] = pool.tile([P, BLOCKS[b][1]], F32, name="acc", tag="acc")
                     cols = slice(P * a, P * a + P)
                     nc.tensor.matmul_mx(
@@ -234,12 +257,17 @@ def tile_moelayer_pa_kernel(tc, x, r, Wg, Wu, Wd, out):
             queue.dma_start(out=out[a][:, BLOCKS[b][0] : BLOCKS[b][0] + BLOCKS[b][1]], in_=y[:])
 
         regrouped = 0
+        pe_regroup(0)
+        pe_done = 1
         for n in range(-1, NU):
             ahead = 1 if n < 0 else min(n, 2)
             while regrouped <= min(n + ahead, NU - 1):
                 regroup(regrouped)
                 if regrouped < 2:
                     x_transposes(regrouped)
+                while pe_done <= min(regrouped + (1 if regrouped < 2 else 2), N_PE - 1):
+                    pe_regroup(pe_done)
+                    pe_done += 1
                 regrouped += 1
             if n < 0:
                 continue
@@ -264,10 +292,10 @@ def tile_moelayer_pa_kernel(tc, x, r, Wg, Wu, Wd, out):
                     y_out(b, 0, nc.scalar.copy, nc.sync)
                 if n == N1 + E * b + E + 1:
                     y_out(b, 1, nc.scalar.copy, nc.sync)
+            if n % 4 == 0 and 4 <= n <= 32:
+                combine((n - 4) // 4, 0)
             if n % 4 == 1 and 5 <= n <= 33:
-                combine((n - 5) // 4, 0)
-            if n % 4 == 2 and 6 <= n <= 34:
-                combine((n - 6) // 4, 1)
-                w_transposes((n - 6) // 4)
+                combine((n - 5) // 4, 1)
+                w_transposes((n - 5) // 4)
         y_out(len(BLOCKS) - 1, 0, nc.vector.tensor_copy, nc.sync)
         y_out(len(BLOCKS) - 1, 1, nc.scalar.copy, nc.scalar)

@@ -22,9 +22,9 @@ N1 = 32
 BLOCKS = ((0, 512), (512, 256), (768, 256))
 NU = N1 + E * len(BLOCKS)
 RAW_BUFS = 16
-CV1 = 240
-CV2 = {512: 256, 256: 128}
-CV2_PE = 208
+CV1 = 248
+CV2 = {512: 264, 256: 136}
+CV2_PE = 216
 N_PE = 38
 PE_COLS = 128
 MANUAL = True

@@ -21,12 +21,13 @@ FLOPS = 2 * NTOK * D * F * E * 2 + 2 * NTOK * E * F * D
 N1 = 32
 BLOCKS = ((0, 512), (512, 256), (768, 256))
 NU = N1 + E * len(BLOCKS)
-RAW_BUFS = 16
+RAW_BUFS = 7
 CV1 = 248
 CV2 = {512: 264, 256: 136}
 CV2_PE = 216
 N_PE = 38
 PE_COLS = 128
+FIRST_MERGED = 6
 MANUAL = True
 
 
@@ -35,11 +36,10 @@ def tile_moelayer_pa_kernel(tc, x, r, Wg, Wu, Wd, out):
     with ExitStack() as ctx:
         const = ctx.enter_context(tc.tile_pool(name="const", bufs=1))
         rawa = ctx.enter_context(tc.tile_pool(name="rawa", bufs=RAW_BUFS))
-        rawd = ctx.enter_context(tc.tile_pool(name="rawd", bufs=E))
-        grp = ctx.enter_context(tc.tile_pool(name="grp", bufs=6))
-        cod = ctx.enter_context(tc.tile_pool(name="cod", bufs=8))
+        grp = ctx.enter_context(tc.tile_pool(name="grp", bufs=4))
+        cod = ctx.enter_context(tc.tile_pool(name="cod", bufs=4))
         act = ctx.enter_context(tc.tile_pool(name="act", bufs=3))
-        yst = ctx.enter_context(tc.tile_pool(name="yst", bufs=6))
+        yst = ctx.enter_context(tc.tile_pool(name="yst", bufs=4))
         psg = ctx.enter_context(tc.psum_pool(name="psg", bufs=2))
         psu = ctx.enter_context(tc.psum_pool(name="psu", bufs=2))
         pst = ctx.enter_context(tc.psum_pool(name="pst", bufs=1))
@@ -50,86 +50,112 @@ def tile_moelayer_pa_kernel(tc, x, r, Wg, Wu, Wd, out):
         raw_tiles = {}
         grp_tiles = {}
         code_tiles = {}
+        ck_tiles = {}
         acc = {}
         sg_tiles = {}
         w_tiles = {}
         wt_tiles = {}
         wg_tiles = {}
-        ck_tiles = {}
 
-        def load(n):
-            if n < N1:
-                e, i = divmod(n, 4)
-                src = (Wg if i < 2 else Wu)[e]
-                c = i % 2
-                t = rawa.tile([P, 4, F], BF16, name="rawa", tag="rawa")
-                nc.sync.dma_start(
-                    out=t[:], in_=src[512 * c : 512 * c + 512, :].rearrange("(p j) f -> p j f", j=4)
-                )
-                raw_tiles[n] = t
-            else:
-                e = n - N1
-                t = rawd.tile([P, 4, D], BF16, name="rawd", tag="rawd")
-                nc.sync.dma_start(out=t[:], in_=Wd[e].rearrange("(t p) d -> p t d", t=4))
-                raw_tiles[n] = t
+        rawd = const.tile([P, E, 4, D], BF16, name="rawd")
+
+        def merged(k):
+            return FIRST_MERGED <= k < NU // 2 - 1
 
         def width(n):
             return F if n < N1 else BLOCKS[(n - N1) // E][1]
 
-        def source(n):
-            if n < N1:
-                return raw_tiles[n][:]
-            b, e = divmod(n - N1, E)
-            return raw_tiles[N1 + e][:, :, BLOCKS[b][0] : BLOCKS[b][0] + BLOCKS[b][1]]
-
         def split(n):
             return CV1 if n < N1 else (CV2_PE if n < N_PE else CV2[width(n)])
 
+        def load(n):
+            k, s = divmod(n, 2)
+            if s == 0:
+                raw_tiles[k] = rawa.tile([P, 2, 4, F], BF16, name="rawa", tag="rawa")
+            src = (Wg if k % 2 == 0 else Wu)[k // 2]
+            nc.sync.dma_start(
+                out=raw_tiles[k][:, s],
+                in_=src[512 * s : 512 * s + 512, :].rearrange("(p j) f -> p j f", j=4),
+            )
+
+        def load_down(e):
+            nc.sync.dma_start(out=rawd[:, e], in_=Wd[e].rearrange("(t p) d -> p t d", t=4))
+
+        def pair_source(k):
+            if 2 * k < N1:
+                return raw_tiles[k][:]
+            b, e = divmod(2 * k - N1, E)
+            return rawd[:, e : e + 2, :, BLOCKS[b][0] : BLOCKS[b][0] + BLOCKS[b][1]]
+
         def pe_regroup(n):
+            k, s = divmod(n, 2)
             cv = split(n)
-            ck = psc.tile([P, PE_COLS, 4], BF16, name="ck", tag="ck")
+            if s == 0:
+                ck_tiles[k] = psc.tile([P, 2, PE_COLS, 4], BF16, name="ck", tag="ck")
             nc.tensor.matmul(
-                out=ck[:].rearrange("p w t -> p t w"),
+                out=ck_tiles[k][:, s].rearrange("p w t -> p t w"),
                 lhsT=ident_b[:],
-                rhs=source(n)[:, :, cv : cv + PE_COLS],
+                rhs=pair_source(k)[:, s, :, cv : cv + PE_COLS],
                 start=True,
                 stop=True,
             )
-            ck_tiles[n] = ck
 
         def regroup(n):
+            k, s = divmod(n, 2)
             w = width(n)
-            g = grp.tile([P, w, 4], BF16, name="grp", tag="grp", align_bytes=64)
-            grp_tiles[n] = g
-            src = source(n)
+            if s == 0:
+                grp_tiles[k] = grp.tile([P, 2, w, 4], BF16, name="grp", tag="grp", align_bytes=64)
+            g = grp_tiles[k]
+            src = pair_source(k)
             cv = split(n)
             cs = cv + PE_COLS if n < N_PE else cv
             nc.scalar.copy(
-                out=g[:, cs:w, :].rearrange("p (c i) t -> p c t i", i=4),
-                in_=src[:, :, cs:w].rearrange("p t (c i) -> p c t i", i=4),
+                out=g[:, s, cs:w, :].rearrange("p (c i) t -> p c t i", i=4),
+                in_=src[:, s, :, cs:w].rearrange("p t (c i) -> p c t i", i=4),
             )
-            if n < N_PE:
-                nc.scalar.copy(out=g[:, cv:cs, :], in_=ck_tiles[n][:])
-            nc.vector.tensor_copy(
-                out=g[:, 0:cv, :].rearrange("p (c i) t -> p c t i", i=4),
-                in_=src[:, :, 0:cv].rearrange("p t (c i) -> p c t i", i=4),
-            )
-            nxt = n + RAW_BUFS
-            if nxt < N1:
-                load(nxt)
-            elif nxt == N1:
-                for e in range(E):
-                    load(N1 + e)
+            if n < N_PE and not merged(k):
+                nc.scalar.copy(out=g[:, s, cv:cs, :], in_=ck_tiles[k][:, s])
+            if n < N_PE and merged(k) and s == 1:
+                nc.scalar.copy(out=g[:, :, cv:cs, :], in_=ck_tiles[k][:])
+            if not merged(k):
+                nc.vector.tensor_copy(
+                    out=g[:, s, 0:cv, :].rearrange("p (c i) t -> p c t i", i=4),
+                    in_=src[:, s, :, 0:cv].rearrange("p t (c i) -> p c t i", i=4),
+                )
+            elif s == 0:
+                nc.vector.tensor_copy(
+                    out=g[:, :, 0:cv, :].rearrange("p s (c i) t -> p s c t i", i=4),
+                    in_=src[:, :, :, 0:cv].rearrange("p s t (c i) -> p s c t i", i=4),
+                )
+            if s == 1:
+                nxt = k + RAW_BUFS
+                if 2 * nxt < N1:
+                    load(2 * nxt)
+                    load(2 * nxt + 1)
+                elif 2 * nxt == N1:
+                    for e in range(E):
+                        load_down(e)
 
         def quantise(n):
-            codes = cod.tile([P, width(n)], U32, name="codes", tag="codes", align_bytes=64)
-            plane = cod.tile([P, width(n)], U8, name="plane", tag="plane", align_bytes=64)
-            nc.vector.quantize_mx(
-                out=codes[:].bitcast(FP8X4),
-                scales=plane[:],
-                in_=grp_tiles[n][:].rearrange("p w t -> p (w t)"),
-            )
-            code_tiles[n] = (codes, plane)
+            k, s = divmod(n, 2)
+            w = width(n)
+            if s == 0:
+                codes = cod.tile([P, 2 * w], U32, name="codes", tag="codes", align_bytes=64)
+                plane = cod.tile([P, 2 * w], U8, name="plane", tag="plane", align_bytes=64)
+                code_tiles[k] = (codes, plane)
+            codes, plane = code_tiles[k]
+            if not merged(k):
+                nc.vector.quantize_mx(
+                    out=codes[:, w * s : w * s + w].bitcast(FP8X4),
+                    scales=plane[:, w * s : w * s + w],
+                    in_=grp_tiles[k][:, s].rearrange("p w t -> p (w t)"),
+                )
+            elif s == 1:
+                nc.vector.quantize_mx(
+                    out=codes[:].bitcast(FP8X4),
+                    scales=plane[:],
+                    in_=grp_tiles[k][:].rearrange("p s w t -> p (s w t)"),
+                )
 
         ident_f = const.tile([P, P], F32, name="ident_f")
         make_identity(nc, ident_f[:])
@@ -143,7 +169,7 @@ def tile_moelayer_pa_kernel(tc, x, r, Wg, Wu, Wd, out):
         x_sb = const.tile([P, 2, D], BF16, name="x_sb")
         load(0)
         nc.sync.dma_start(out=x_sb[:], in_=x.rearrange("b t d -> t b d"))
-        for n in range(1, RAW_BUFS):
+        for n in range(1, 2 * RAW_BUFS):
             load(n)
 
         r32 = const.tile([P, 2, E], F32, name="r32")
@@ -175,7 +201,10 @@ def tile_moelayer_pa_kernel(tc, x, r, Wg, Wu, Wd, out):
             )
 
         def matmuls(n):
-            codes, plane = code_tiles[n]
+            k, s = divmod(n, 2)
+            w = width(n)
+            codes, plane = code_tiles[k]
+            mov = slice(w * s, w * s + w)
             if n < N1:
                 e, i = divmod(n, 4)
                 c = i % 2
@@ -188,8 +217,8 @@ def tile_moelayer_pa_kernel(tc, x, r, Wg, Wu, Wd, out):
                         out=acc[(i // 2, e, a)][:],
                         lhsT=xc[:, cols].bitcast(FP8X4),
                         lhsT_scale=xs[:, cols],
-                        rhs=codes[:].bitcast(FP8X4),
-                        rhs_scale=plane[:],
+                        rhs=codes[:, mov].bitcast(FP8X4),
+                        rhs_scale=plane[:, mov],
                         start=(c == 0),
                         stop=(c == 1),
                     )
@@ -198,14 +227,14 @@ def tile_moelayer_pa_kernel(tc, x, r, Wg, Wu, Wd, out):
                 for a in range(2):
                     if e == 0:
                         pool = (psg, psu, psg)[b]
-                        acc[(2 + b, 0, a)] = pool.tile([P, BLOCKS[b][1]], F32, name="acc", tag="acc")
+                        acc[(2 + b, 0, a)] = pool.tile([P, w], F32, name="acc", tag="acc")
                     cols = slice(P * a, P * a + P)
                     nc.tensor.matmul_mx(
                         out=acc[(2 + b, 0, a)][:],
                         lhsT=wc[:, e, cols].bitcast(FP8X4),
                         lhsT_scale=ws[:, e, cols],
-                        rhs=codes[:].bitcast(FP8X4),
-                        rhs_scale=plane[:],
+                        rhs=codes[:, mov].bitcast(FP8X4),
+                        rhs_scale=plane[:, mov],
                         start=(e == 0),
                         stop=(e == E - 1),
                     )
@@ -265,7 +294,7 @@ def tile_moelayer_pa_kernel(tc, x, r, Wg, Wu, Wd, out):
                 regroup(regrouped)
                 if regrouped < 2:
                     x_transposes(regrouped)
-                while pe_done <= min(regrouped + (1 if regrouped < 2 else 2), N_PE - 1):
+                while pe_done <= min(regrouped + (1 if regrouped < 2 * FIRST_MERGED - 2 else 3), N_PE - 1):
                     pe_regroup(pe_done)
                     pe_done += 1
                 regrouped += 1
@@ -277,7 +306,11 @@ def tile_moelayer_pa_kernel(tc, x, r, Wg, Wu, Wd, out):
                 matmuls(0)
             if n % 4 == 3 and 11 <= n <= 39:
                 w_quantise((n - 11) // 4)
-            if n >= 1:
+            if not merged(n // 2):
+                if n >= 1:
+                    matmuls(n)
+            elif n % 2 == 1:
+                matmuls(n - 1)
                 matmuls(n)
             if n < N1 and n % 4 == 2:
                 silu(n // 4, 0)

@@ -21,13 +21,12 @@ FLOPS = 2 * NTOK * D * F * E * 2 + 2 * NTOK * E * F * D
 N1 = 32
 BLOCKS = ((0, 512), (512, 256), (768, 256))
 NU = N1 + E * len(BLOCKS)
-RAW_BUFS = 7
+RAW_BUFS = 16
 CV1 = 248
 CV2 = {512: 264, 256: 136}
 CV2_PE = 216
 N_PE = 38
 PE_COLS = 128
-FIRST_MERGED = 6
 MANUAL = True
 
 
@@ -36,126 +35,101 @@ def tile_moelayer_pa_kernel(tc, x, r, Wg, Wu, Wd, out):
     with ExitStack() as ctx:
         const = ctx.enter_context(tc.tile_pool(name="const", bufs=1))
         rawa = ctx.enter_context(tc.tile_pool(name="rawa", bufs=RAW_BUFS))
-        grp = ctx.enter_context(tc.tile_pool(name="grp", bufs=4))
-        cod = ctx.enter_context(tc.tile_pool(name="cod", bufs=4))
+        rawd = ctx.enter_context(tc.tile_pool(name="rawd", bufs=E))
+        grp = ctx.enter_context(tc.tile_pool(name="grp", bufs=6))
+        cod = ctx.enter_context(tc.tile_pool(name="cod", bufs=8))
         act = ctx.enter_context(tc.tile_pool(name="act", bufs=3))
-        yst = ctx.enter_context(tc.tile_pool(name="yst", bufs=4))
+        yst = ctx.enter_context(tc.tile_pool(name="yst", bufs=6))
         psg = ctx.enter_context(tc.psum_pool(name="psg", bufs=2))
         psu = ctx.enter_context(tc.psum_pool(name="psu", bufs=2))
-        pst = ctx.enter_context(tc.psum_pool(name="pst", bufs=1))
-        psc = ctx.enter_context(tc.psum_pool(name="psc", bufs=3))
+        pst = ctx.enter_context(tc.psum_pool(name="pst", bufs=2))
+        psc = ctx.enter_context(tc.psum_pool(name="psc", bufs=2))
         if MANUAL:
             ctx.enter_context(tc.manual_schedule())
 
         raw_tiles = {}
         grp_tiles = {}
         code_tiles = {}
-        ck_tiles = {}
         acc = {}
         sg_tiles = {}
         w_tiles = {}
         wt_tiles = {}
         wg_tiles = {}
+        ck_tiles = {}
 
-        rawd = const.tile([P, E, 4, D], BF16, name="rawd")
-
-        def merged(k):
-            return FIRST_MERGED <= k < NU // 2 - 1
+        def load(n):
+            if n < N1:
+                e, i = divmod(n, 4)
+                src = (Wg if i < 2 else Wu)[e]
+                c = i % 2
+                t = rawa.tile([P, 4, F], BF16, name="rawa", tag="rawa")
+                nc.sync.dma_start(
+                    out=t[:], in_=src[512 * c : 512 * c + 512, :].rearrange("(p j) f -> p j f", j=4)
+                )
+                raw_tiles[n] = t
+            else:
+                e = n - N1
+                t = rawd.tile([P, 4, D], BF16, name="rawd", tag="rawd")
+                nc.sync.dma_start(out=t[:], in_=Wd[e].rearrange("(t p) d -> p t d", t=4))
+                raw_tiles[n] = t
 
         def width(n):
             return F if n < N1 else BLOCKS[(n - N1) // E][1]
 
+        def source(n):
+            if n < N1:
+                return raw_tiles[n][:]
+            b, e = divmod(n - N1, E)
+            return raw_tiles[N1 + e][:, :, BLOCKS[b][0] : BLOCKS[b][0] + BLOCKS[b][1]]
+
         def split(n):
             return CV1 if n < N1 else (CV2_PE if n < N_PE else CV2[width(n)])
 
-        def load(n):
-            k, s = divmod(n, 2)
-            if s == 0:
-                raw_tiles[k] = rawa.tile([P, 2, 4, F], BF16, name="rawa", tag="rawa")
-            src = (Wg if k % 2 == 0 else Wu)[k // 2]
-            nc.sync.dma_start(
-                out=raw_tiles[k][:, s],
-                in_=src[512 * s : 512 * s + 512, :].rearrange("(p j) f -> p j f", j=4),
-            )
-
-        def load_down(e):
-            nc.sync.dma_start(out=rawd[:, e], in_=Wd[e].rearrange("(t p) d -> p t d", t=4))
-
-        def pair_source(k):
-            if 2 * k < N1:
-                return raw_tiles[k][:]
-            b, e = divmod(2 * k - N1, E)
-            return rawd[:, e : e + 2, :, BLOCKS[b][0] : BLOCKS[b][0] + BLOCKS[b][1]]
-
         def pe_regroup(n):
-            k, s = divmod(n, 2)
             cv = split(n)
-            if s == 0:
-                ck_tiles[k] = psc.tile([P, 2, PE_COLS, 4], BF16, name="ck", tag="ck")
+            ck = psc.tile([P, PE_COLS, 4], BF16, name="ck", tag="ck")
             nc.tensor.matmul(
-                out=ck_tiles[k][:, s].rearrange("p w t -> p t w"),
+                out=ck[:].rearrange("p w t -> p t w"),
                 lhsT=ident_b[:],
-                rhs=pair_source(k)[:, s, :, cv : cv + PE_COLS],
+                rhs=source(n)[:, :, cv : cv + PE_COLS],
                 start=True,
                 stop=True,
             )
+            ck_tiles[n] = ck
 
         def regroup(n):
-            k, s = divmod(n, 2)
             w = width(n)
-            if s == 0:
-                grp_tiles[k] = grp.tile([P, 2, w, 4], BF16, name="grp", tag="grp", align_bytes=64)
-            g = grp_tiles[k]
-            src = pair_source(k)
+            g = grp.tile([P, w, 4], BF16, name="grp", tag="grp", align_bytes=64)
+            grp_tiles[n] = g
+            src = source(n)
             cv = split(n)
             cs = cv + PE_COLS if n < N_PE else cv
             nc.scalar.copy(
-                out=g[:, s, cs:w, :].rearrange("p (c i) t -> p c t i", i=4),
-                in_=src[:, s, :, cs:w].rearrange("p t (c i) -> p c t i", i=4),
+                out=g[:, cs:w, :].rearrange("p (c i) t -> p c t i", i=4),
+                in_=src[:, :, cs:w].rearrange("p t (c i) -> p c t i", i=4),
             )
-            if n < N_PE and not merged(k):
-                nc.scalar.copy(out=g[:, s, cv:cs, :], in_=ck_tiles[k][:, s])
-            if n < N_PE and merged(k) and s == 1:
-                nc.scalar.copy(out=g[:, :, cv:cs, :], in_=ck_tiles[k][:])
-            if not merged(k):
-                nc.vector.tensor_copy(
-                    out=g[:, s, 0:cv, :].rearrange("p (c i) t -> p c t i", i=4),
-                    in_=src[:, s, :, 0:cv].rearrange("p t (c i) -> p c t i", i=4),
-                )
-            elif s == 0:
-                nc.vector.tensor_copy(
-                    out=g[:, :, 0:cv, :].rearrange("p s (c i) t -> p s c t i", i=4),
-                    in_=src[:, :, :, 0:cv].rearrange("p s t (c i) -> p s c t i", i=4),
-                )
-            if s == 1:
-                nxt = k + RAW_BUFS
-                if 2 * nxt < N1:
-                    load(2 * nxt)
-                    load(2 * nxt + 1)
-                elif 2 * nxt == N1:
-                    for e in range(E):
-                        load_down(e)
+            if n < N_PE:
+                nc.scalar.copy(out=g[:, cv:cs, :], in_=ck_tiles[n][:])
+            nc.vector.tensor_copy(
+                out=g[:, 0:cv, :].rearrange("p (c i) t -> p c t i", i=4),
+                in_=src[:, :, 0:cv].rearrange("p t (c i) -> p c t i", i=4),
+            )
+            nxt = n + RAW_BUFS
+            if nxt < N1:
+                load(nxt)
+            elif nxt == N1:
+                for e in range(E):
+                    load(N1 + e)
 
         def quantise(n):
-            k, s = divmod(n, 2)
-            w = width(n)
-            if s == 0:
-                codes = cod.tile([P, 2 * w], U32, name="codes", tag="codes", align_bytes=64)
-                plane = cod.tile([P, 2 * w], U8, name="plane", tag="plane", align_bytes=64)
-                code_tiles[k] = (codes, plane)
-            codes, plane = code_tiles[k]
-            if not merged(k):
-                nc.vector.quantize_mx(
-                    out=codes[:, w * s : w * s + w].bitcast(FP8X4),
-                    scales=plane[:, w * s : w * s + w],
-                    in_=grp_tiles[k][:, s].rearrange("p w t -> p (w t)"),
-                )
-            elif s == 1:
-                nc.vector.quantize_mx(
-                    out=codes[:].bitcast(FP8X4),
-                    scales=plane[:],
-                    in_=grp_tiles[k][:].rearrange("p s w t -> p (s w t)"),
-                )
+            codes = cod.tile([P, width(n)], U32, name="codes", tag="codes", align_bytes=64)
+            plane = cod.tile([P, width(n)], U8, name="plane", tag="plane", align_bytes=64)
+            nc.vector.quantize_mx(
+                out=codes[:].bitcast(FP8X4),
+                scales=plane[:],
+                in_=grp_tiles[n][:].rearrange("p w t -> p (w t)"),
+            )
+            code_tiles[n] = (codes, plane)
 
         ident_f = const.tile([P, P], F32, name="ident_f")
         make_identity(nc, ident_f[:])
@@ -169,7 +143,7 @@ def tile_moelayer_pa_kernel(tc, x, r, Wg, Wu, Wd, out):
         x_sb = const.tile([P, 2, D], BF16, name="x_sb")
         load(0)
         nc.sync.dma_start(out=x_sb[:], in_=x.rearrange("b t d -> t b d"))
-        for n in range(1, 2 * RAW_BUFS):
+        for n in range(1, RAW_BUFS):
             load(n)
 
         r32 = const.tile([P, 2, E], F32, name="r32")
@@ -201,10 +175,7 @@ def tile_moelayer_pa_kernel(tc, x, r, Wg, Wu, Wd, out):
             )
 
         def matmuls(n):
-            k, s = divmod(n, 2)
-            w = width(n)
-            codes, plane = code_tiles[k]
-            mov = slice(w * s, w * s + w)
+            codes, plane = code_tiles[n]
             if n < N1:
                 e, i = divmod(n, 4)
                 c = i % 2
@@ -217,8 +188,8 @@ def tile_moelayer_pa_kernel(tc, x, r, Wg, Wu, Wd, out):
                         out=acc[(i // 2, e, a)][:],
                         lhsT=xc[:, cols].bitcast(FP8X4),
                         lhsT_scale=xs[:, cols],
-                        rhs=codes[:, mov].bitcast(FP8X4),
-                        rhs_scale=plane[:, mov],
+                        rhs=codes[:].bitcast(FP8X4),
+                        rhs_scale=plane[:],
                         start=(c == 0),
                         stop=(c == 1),
                     )
@@ -227,14 +198,14 @@ def tile_moelayer_pa_kernel(tc, x, r, Wg, Wu, Wd, out):
                 for a in range(2):
                     if e == 0:
                         pool = (psg, psu, psg)[b]
-                        acc[(2 + b, 0, a)] = pool.tile([P, w], F32, name="acc", tag="acc")
+                        acc[(2 + b, 0, a)] = pool.tile([P, BLOCKS[b][1]], F32, name="acc", tag="acc")
                     cols = slice(P * a, P * a + P)
                     nc.tensor.matmul_mx(
                         out=acc[(2 + b, 0, a)][:],
                         lhsT=wc[:, e, cols].bitcast(FP8X4),
                         lhsT_scale=ws[:, e, cols],
-                        rhs=codes[:, mov].bitcast(FP8X4),
-                        rhs_scale=plane[:, mov],
+                        rhs=codes[:].bitcast(FP8X4),
+                        rhs_scale=plane[:],
                         start=(e == 0),
                         stop=(e == E - 1),
                     )
@@ -294,7 +265,7 @@ def tile_moelayer_pa_kernel(tc, x, r, Wg, Wu, Wd, out):
                 regroup(regrouped)
                 if regrouped < 2:
                     x_transposes(regrouped)
-                while pe_done <= min(regrouped + (1 if regrouped < 2 * FIRST_MERGED - 2 else 3), N_PE - 1):
+                while pe_done <= min(regrouped + 1, N_PE - 1):
                     pe_regroup(pe_done)
                     pe_done += 1
                 regrouped += 1
@@ -306,11 +277,7 @@ def tile_moelayer_pa_kernel(tc, x, r, Wg, Wu, Wd, out):
                 matmuls(0)
             if n % 4 == 3 and 11 <= n <= 39:
                 w_quantise((n - 11) // 4)
-            if not merged(n // 2):
-                if n >= 1:
-                    matmuls(n)
-            elif n % 2 == 1:
-                matmuls(n - 1)
+            if n >= 1:
                 matmuls(n)
             if n < N1 and n % 4 == 2:
                 silu(n // 4, 0)
@@ -321,9 +288,9 @@ def tile_moelayer_pa_kernel(tc, x, r, Wg, Wu, Wd, out):
             if n % 4 == 1 and 9 <= n <= 37:
                 w_copy((n - 9) // 4, 1)
             for b in range(len(BLOCKS) - 1):
-                if n == N1 + E * b + E:
-                    y_out(b, 0, nc.scalar.copy, nc.sync)
                 if n == N1 + E * b + E + 1:
+                    y_out(b, 0, nc.scalar.copy, nc.sync)
+                if n == N1 + E * b + E + 2:
                     y_out(b, 1, nc.scalar.copy, nc.sync)
             if n % 4 == 0 and 4 <= n <= 32:
                 combine((n - 4) // 4, 0)

from contextlib import ExitStack

import concourse.mybir as mybir
from concourse.masks import make_identity

F32 = mybir.dt.float32
BF16 = mybir.dt.bfloat16
U32 = mybir.dt.uint32
U8 = mybir.dt.uint8
FP8X4 = mybir.dt.float8_e4m3fn_x4
SILU = mybir.ActivationFunctionType.Silu
MULT = mybir.AluOpType.mult

P = 128
E = 8
D = 1024
F = 512
NTOK = 256
FLOPS = 2 * NTOK * D * F * E * 2 + 2 * NTOK * E * F * D

N1 = 32
BLOCKS = ((0, 512), (512, 256), (768, 256))
NU = N1 + E * len(BLOCKS)
RAW_BUFS = 16
CV1 = 248
CV2 = {512: 264, 256: 136}
CV2_PE = 216
N_PE = 38
PE_COLS = 128
MANUAL = True


def tile_moelayer_pa_kernel(tc, x, r, Wg, Wu, Wd, out):
    nc = tc.nc
    with ExitStack() as ctx:
        const = ctx.enter_context(tc.tile_pool(name="const", bufs=1))
        rawa = ctx.enter_context(tc.tile_pool(name="rawa", bufs=RAW_BUFS))
        rawd = ctx.enter_context(tc.tile_pool(name="rawd", bufs=E))
        grp = ctx.enter_context(tc.tile_pool(name="grp", bufs=6))
        cod = ctx.enter_context(tc.tile_pool(name="cod", bufs=8))
        act = ctx.enter_context(tc.tile_pool(name="act", bufs=3))
        yst = ctx.enter_context(tc.tile_pool(name="yst", bufs=6))
        psg = ctx.enter_context(tc.psum_pool(name="psg", bufs=2))
        psu = ctx.enter_context(tc.psum_pool(name="psu", bufs=2))
        pst = ctx.enter_context(tc.psum_pool(name="pst", bufs=2))
        psc = ctx.enter_context(tc.psum_pool(name="psc", bufs=2))
        if MANUAL:
            ctx.enter_context(tc.manual_schedule())

        raw_tiles = {}
        grp_tiles = {}
        code_tiles = {}
        acc = {}
        sg_tiles = {}
        w_tiles = {}
        wt_tiles = {}
        wg_tiles = {}
        ck_tiles = {}

        def load(n):
            if n < N1:
                e, i = divmod(n, 4)
                src = (Wg if i < 2 else Wu)[e]
                c = i % 2
                t = rawa.tile([P, 4, F], BF16, name="rawa", tag="rawa")
                nc.sync.dma_start(
                    out=t[:], in_=src[512 * c : 512 * c + 512, :].rearrange("(p j) f -> p j f", j=4)
                )
                raw_tiles[n] = t
            else:
                e = n - N1
                t = rawd.tile([P, 4, D], BF16, name="rawd", tag="rawd")
                nc.sync.dma_start(out=t[:], in_=Wd[e].rearrange("(t p) d -> p t d", t=4))
                raw_tiles[n] = t

        def width(n):
            return F if n < N1 else BLOCKS[(n - N1) // E][1]

        def source(n):
            if n < N1:
                return raw_tiles[n][:]
            b, e = divmod(n - N1, E)
            return raw_tiles[N1 + e][:, :, BLOCKS[b][0] : BLOCKS[b][0] + BLOCKS[b][1]]

        def split(n):
            return CV1 if n < N1 else (CV2_PE if n < N_PE else CV2[width(n)])

        def pe_regroup(n):
            cv = split(n)
            ck = psc.tile([P, PE_COLS, 4], BF16, name="ck", tag="ck")
            nc.tensor.matmul(
                out=ck[:].rearrange("p w t -> p t w"),
                lhsT=ident_b[:],
                rhs=source(n)[:, :, cv : cv + PE_COLS],
                start=True,
                stop=True,
            )
            ck_tiles[n] = ck

        def regroup(n):
            w = width(n)
            g = grp.tile([P, w, 4], BF16, name="grp", tag="grp", align_bytes=64)
            grp_tiles[n] = g
            src = source(n)
            cv = split(n)
            cs = cv + PE_COLS if n < N_PE else cv
            nc.scalar.copy(
                out=g[:, cs:w, :].rearrange("p (c i) t -> p c t i", i=4),
                in_=src[:, :, cs:w].rearrange("p t (c i) -> p c t i", i=4),
            )
            if n < N_PE:
                nc.scalar.copy(out=g[:, cv:cs, :], in_=ck_tiles[n][:])
            nc.vector.tensor_copy(
                out=g[:, 0:cv, :].rearrange("p (c i) t -> p c t i", i=4),
                in_=src[:, :, 0:cv].rearrange("p t (c i) -> p c t i", i=4),
            )
            nxt = n + RAW_BUFS
            if nxt < N1:
                load(nxt)
            elif nxt == N1:
                for e in range(E):
                    load(N1 + e)

        def quantise(n):
            codes = cod.tile([P, width(n)], U32, name="codes", tag="codes", align_bytes=64)
            plane = cod.tile([P, width(n)], U8, name="plane", tag="plane", align_bytes=64)
            nc.vector.quantize_mx(
                out=codes[:].bitcast(FP8X4),
                scales=plane[:],
                in_=grp_tiles[n][:].rearrange("p w t -> p (w t)"),
            )
            code_tiles[n] = (codes, plane)

        ident_f = const.tile([P, P], F32, name="ident_f")
        make_identity(nc, ident_f[:])
        ident_b = const.tile([P, P], BF16, name="ident_b")
        make_identity(nc, ident_b[:])
        r_sb = const.tile([P, 2, E], BF16, name="r_sb")
        nc.scalar.dma_start(out=r_sb[:], in_=r.rearrange("(a p) e -> p a e", a=2))
        warm = const.tile([P, 1], F32, name="warm")
        nc.vector.memset(warm[:], 0.0)
        nc.scalar.activation(out=warm[:], in_=warm[:], func=SILU)
        x_sb = const.tile([P, 2, D], BF16, name="x_sb")
        load(0)
        nc.sync.dma_start(out=x_sb[:], in_=x.rearrange("b t d -> t b d"))
        for n in range(1, RAW_BUFS):
            load(n)

        r32 = const.tile([P, 2, E], F32, name="r32")
        nc.vector.tensor_copy(out=r32[:], in_=r_sb[:])

        xg = const.tile([P, 2, NTOK, 4], BF16, name="xg", align_bytes=64)
        xc = const.tile([P, 2 * NTOK], U32, name="xc", align_bytes=64)
        xs = const.tile([P, 2 * NTOK], U8, name="xs", align_bytes=64)
        wc = const.tile([P, E, NTOK], U32, name="wc", align_bytes=64)
        ws = const.tile([P, E, NTOK], U8, name="ws", align_bytes=64)

        def x_transposes(c):
            xw = x_sb[:].bitcast(F32).rearrange("p a (c q u) -> p a c u q", c=2, u=2)
            xg32 = xg[:].bitcast(F32)
            xt = pst.tile([P, 2, 2, P], F32, name="xt", tag="tp")
            for a in range(2):
                for u in range(2):
                    nc.tensor.transpose(out=xt[:, a, u, :], in_=xw[:, a, c, u, :], identity=ident_f[:])
            nc.scalar.copy(
                out=xg32[:, c].rearrange("p (a q) u -> p a q u", a=2),
                in_=xt[:].rearrange("p a u q -> p a q u"),
            )

        def x_quantise():
            nc.vector.quantize_mx(
                out=xc[:].bitcast(FP8X4),
                scales=xs[:],
                in_=xg[:].rearrange("p c n t -> p (c n t)"),
            )

        def matmuls(n):
            codes, plane = code_tiles[n]
            if n < N1:
                e, i = divmod(n, 4)
                c = i % 2
                for a in range(2):
                    if c == 0:
                        pool = psg if i < 2 else psu
                        acc[(i // 2, e, a)] = pool.tile([P, F], F32, name="acc", tag="acc")
                    cols = slice(NTOK * c + P * a, NTOK * c + P * a + P)
                    nc.tensor.matmul_mx(
                        out=acc[(i // 2, e, a)][:],
                        lhsT=xc[:, cols].bitcast(FP8X4),
                        lhsT_scale=xs[:, cols],
                        rhs=codes[:].bitcast(FP8X4),
                        rhs_scale=plane[:],
                        start=(c == 0),
                        stop=(c == 1),
                    )
            else:
                b, e = divmod(n - N1, E)
                for a in range(2):
                    if e == 0:
                        pool = (psg, psu, psg)[b]
                        acc[(2 + b, 0, a)] = pool.tile([P, BLOCKS[b][1]], F32, name="acc", tag="acc")
                    cols = slice(P * a, P * a + P)
                    nc.tensor.matmul_mx(
                        out=acc[(2 + b, 0, a)][:],
                        lhsT=wc[:, e, cols].bitcast(FP8X4),
                        lhsT_scale=ws[:, e, cols],
                        rhs=codes[:].bitcast(FP8X4),
                        rhs_scale=plane[:],
                        start=(e == 0),
                        stop=(e == E - 1),
                    )

        def silu(e, a):
            sg = act.tile([P, F], F32, name="sg", tag="sg")
            nc.scalar.activation(out=sg[:], in_=acc[(0, e, a)][:], func=SILU)
            sg_tiles[(e, a)] = sg

        def combine(e, a):
            w = act.tile([P, F], BF16, name="w", tag="w")
            nc.vector.scalar_tensor_tensor(
                out=w[:],
                in0=sg_tiles[(e, a)][:],
                scalar=r32[:, a, e : e + 1],
                in1=acc[(1, e, a)][:],
                op0=MULT,
                op1=MULT,
            )
            w_tiles[(e, a)] = w

        def w_transposes(e):
            wt = pst.tile([P, 2, 4, P], BF16, name="wt", tag="tp")
            for a in range(2):
                for t in range(4):
                    nc.tensor.transpose(
                        out=wt[:, a, t, :], in_=w_tiles[(e, a)][:, P * t : P * t + P], identity=ident_b[:]
                    )
            wt_tiles[e] = wt

        def w_copy(e, a):
            if a == 0:
                wg_tiles[e] = act.tile([P, NTOK, 4], BF16, name="wg", tag="wg", align_bytes=64)
            nc.scalar.copy(
                out=wg_tiles[e][:, P * a : P * a + P, :],
                in_=wt_tiles[e][:, a].rearrange("p t q -> p q t"),
            )

        def w_quantise(e):
            nc.vector.quantize_mx(
                out=wc[:, e, :].bitcast(FP8X4),
                scales=ws[:, e, :],
                in_=wg_tiles[e][:].rearrange("p n t -> p (n t)"),
            )

        def y_out(b, a, copy, queue):
            y = yst.tile([P, BLOCKS[b][1]], F32, name="y", tag="y")
            copy(out=y[:], in_=acc[(2 + b, 0, a)][:])
            queue.dma_start(out=out[a][:, BLOCKS[b][0] : BLOCKS[b][0] + BLOCKS[b][1]], in_=y[:])

        regrouped = 0
        pe_regroup(0)
        pe_done = 1
        for n in range(-1, NU):
            ahead = 1 if n < 0 else min(n, 2)
            while regrouped <= min(n + ahead, NU - 1):
                regroup(regrouped)
                if regrouped < 2:
                    x_transposes(regrouped)
                while pe_done <= min(regrouped + 1, N_PE - 1):
                    pe_regroup(pe_done)
                    pe_done += 1
                regrouped += 1
            if n < 0:
                continue
            quantise(n)
            if n == 1:
                x_quantise()
                matmuls(0)
            if n % 4 == 3 and 11 <= n <= 39:
                w_quantise((n - 11) // 4)
            if n >= 1:
                matmuls(n)
            if n < N1 and n % 4 == 2:
                silu(n // 4, 0)
            if n < N1 and n % 4 == 3:
                silu(n // 4, 1)
            if n % 4 == 0 and 8 <= n <= 36:
                w_copy((n - 8) // 4, 0)
            if n % 4 == 1 and 9 <= n <= 37:
                w_copy((n - 9) // 4, 1)
            for b in range(len(BLOCKS) - 1):
                if n == N1 + E * b + E + 1:
                    y_out(b, 0, nc.scalar.copy, nc.sync)
                if n == N1 + E * b + E + 2:
                    y_out(b, 1, nc.scalar.copy, nc.sync)
            if n % 4 == 0 and 4 <= n <= 32:
                combine((n - 4) // 4, 0)
            if n % 4 == 1 and 5 <= n <= 33:
                combine((n - 5) // 4, 1)
                w_transposes((n - 5) // 4)
        y_out(len(BLOCKS) - 1, 0, nc.vector.tensor_copy, nc.sync)
        y_out(len(BLOCKS) - 1, 1, nc.scalar.copy, nc.scalar)
